import numpy as np
import ml_dtypes


def mxq(x, axis, fmt="e4m3"):
    dtype, down = {"e4m3": (ml_dtypes.float8_e4m3fn, 7), "e5m2": (ml_dtypes.float8_e5m2, 14)}[fmt]
    v = np.moveaxis(np.asarray(x, np.float32).astype(ml_dtypes.bfloat16).astype(np.float64), axis, -1)
    blocks = v.reshape(v.shape[:-1] + (-1, 32))
    amax = np.abs(blocks).max(-1, keepdims=True)
    byte = np.maximum(np.where(amax > 0, np.frexp(amax)[1] - 1 + 127, 0) - down, 1)
    scale = np.exp2(byte - 127.0)
    codes = (blocks / scale).astype(np.float32).astype(dtype).astype(np.float64)
    return np.moveaxis((codes * scale).reshape(v.shape), -1, axis)


WIDE = False


def mx_kscale(k):
    if not WIDE:
        return np.ones(k)
    levels = np.array([10, -10, 5, -5, 0])
    if k % 512:
        return np.exp2(np.random.permutation(np.resize(levels, k // 32))).repeat(32)
    a = np.empty((k // 512, 16))
    for p in range(k // 512):
        a[p, :8] = np.random.permutation(np.resize(levels, 8))
        for g in range(8):
            far = levels[np.abs(levels - a[p, g]) >= 10]
            a[p, g + 8] = far[np.random.randint(len(far))]
    return np.exp2(a.ravel()).repeat(32)


BF16 = ml_dtypes.bfloat16


def bf(x):
    return np.asarray(x, np.float32).astype(BF16)


def f64(x):
    return np.asarray(x).astype(np.float64)


B, T, D, M, C = 8, 512, 512, 2, 512
MD = M * D
LN_EPS = 1e-5


def draw0():
    s, t = mx_kscale(T), mx_kscale(MD)
    sc = np.random.standard_normal((B, M, T, T)) * 2.0
    sc = np.where(np.tril(np.ones((T, T), dtype=bool)), sc, -np.inf)
    e = np.exp(sc - sc.max(-1, keepdims=True))
    attn = e / e.sum(-1, keepdims=True)
    return {"attn": bf(attn * s),
            "pz": bf(np.random.standard_normal((B, M, T, D)) / s[:, None] * t.reshape(M, 1, D)),
            "Wo": bf(np.random.standard_normal((D, MD)) * 2.0 / np.sqrt(MD) / t),
            "bo": bf(np.random.standard_normal(D) * 0.3),
            "x": bf(np.random.standard_normal((B, T, D))),
            "gamma": bf(1.0 + 0.1 * np.random.standard_normal(D)),
            "beta": bf(0.1 * np.random.standard_normal(D))}


def core(attn, pz, Wo, bo, x, gamma, beta):
    a = f64(attn)
    pq = mxq(f64(pz), 2, "e4m3")
    rows = []
    for r in range(0, T, C):
        aq = mxq(a[:, :, r:r + C, :r + C], 3, "e4m3")
        rows.append(aq @ pq[:, :, :r + C, :])
    out = np.concatenate(rows, axis=2)
    cat = out.transpose(0, 2, 1, 3).reshape(B, T, MD)
    y = (mxq(cat, 2, "e4m3") @ mxq(f64(Wo), 1, "e4m3").T) + f64(bo)
    h = y + f64(x)
    mu = h.mean(-1, keepdims=True)
    var = h.var(-1, keepdims=True)
    return (h - mu) / np.sqrt(var + LN_EPS) * f64(gamma) + f64(beta)


def e4m3fn_bytes(y):
    return np.clip(np.asarray(y, np.float64), -448.0, 448.0).astype(np.float32).astype(ml_dtypes.float8_e4m3fn).view(np.uint8)


def e4m3fn_values(b):
    return np.asarray(b, np.uint8).view(ml_dtypes.float8_e4m3fn).astype(np.float64)


def setup_inputs():
    d = draw0()
    x0 = np.asarray(d['Wo']).astype(np.float64)
    s = (np.max(np.abs(x0), axis=(0,), keepdims=True) / 448.0).astype(np.float32)
    out = {}
    for k, v in d.items():
        if k == 'Wo':
            out['Wo_bytes'] = e4m3fn_bytes(x0 / s.astype(np.float64))
            out['Wo_scale'] = s
        else:
            out[k] = v
    return out


def reference(attn, pz, Wo_bytes, Wo_scale, bo, x, gamma, beta):
    return core(attn, pz, e4m3fn_values(Wo_bytes) * Wo_scale.astype(np.float64), bo, x, gamma, beta)

@@ -1,0 +1,257 @@
+from contextlib import ExitStack
+
+import concourse.mybir as mybir
+from concourse.masks import make_identity
+
+B, HEADS, T, D = 8, 2, 512, 512
+FLOPS = 2 * B * HEADS * T * T * D + 2 * B * T * HEADS * D * D
+
+F32 = mybir.dt.float32
+BF16 = mybir.dt.bfloat16
+U32 = mybir.dt.uint32
+U8 = mybir.dt.uint8
+FP8 = mybir.dt.float8_e4m3fn
+FP8X4 = mybir.dt.float8_e4m3fn_x4
+ALU = mybir.AluOpType
+ACT = mybir.ActivationFunctionType
+
+P = 128
+N_HEADS = B * HEADS
+V_HEADS = (0,)
+S_HEADS = (5, 9, 13)
+LEAD = 4
+
+
+def tile_softmaxattention_pb_t_kernel(tc, attn, pz, Wo_bytes, Wo_scale, bo, x, gamma, beta, out):
+    nc = tc.nc
+    with ExitStack() as ctx:
+        const = ctx.enter_context(tc.tile_pool(name="const", bufs=1))
+        raw = ctx.enter_context(tc.tile_pool(name="raw", bufs=6))
+        grp = ctx.enter_context(tc.tile_pool(name="grp", bufs=3))
+        codes = ctx.enter_context(tc.tile_pool(name="codes", bufs=3))
+        ccodes = ctx.enter_context(tc.tile_pool(name="ccodes", bufs=5))
+        post = ctx.enter_context(tc.tile_pool(name="post", bufs=3))
+        small = ctx.enter_context(tc.tile_pool(name="small", bufs=4))
+        ps_tr = ctx.enter_context(tc.psum_pool(name="ps_tr", bufs=2))
+        ps_cat = ctx.enter_context(tc.psum_pool(name="ps_cat", bufs=2))
+        ps_y = ctx.enter_context(tc.psum_pool(name="ps_y", bufs=2))
+        ps_pz = ctx.enter_context(tc.psum_pool(name="ps_pz", bufs=2))
+
+        ident_f = const.tile([P, P], F32, align_bytes=64)
+        ident_b = const.tile([P, P], BF16, align_bytes=64)
+        make_identity(nc, ident_f[:])
+        make_identity(nc, ident_b[:])
+
+        wo_raw = const.tile([P, 4, HEADS * D], U8, align_bytes=64)
+        wo_sc = const.tile([P, HEADS, 4], F32, align_bytes=64)
+        wo_wide = const.tile([P, 4, HEADS * D], BF16, align_bytes=64)
+        wo_grp = const.tile([P, HEADS, D, 4], BF16, align_bytes=64)
+        wo_codes = const.tile([P, HEADS, D], U32, align_bytes=64)
+        wo_scales = const.tile([P, HEADS, D], U8, align_bytes=64)
+        bo_t = const.tile([P, D], BF16, align_bytes=64)
+        gamma_t = const.tile([P, D], BF16, align_bytes=64)
+        beta_t = const.tile([P, D], BF16, align_bytes=64)
+
+        attn_h = attn.rearrange("b m (p j) s -> (b m) p (j s)", j=4)
+        pz_h = pz.rearrange("b m (p j) i -> (b m) p (j i)", j=4)
+        x_b = x.rearrange("b (p j) o -> b p j o", j=4)
+        out_b = out.rearrange("b (p j) o -> b p j o", j=4)
+
+        st = {}
+
+        def load_pz(n):
+            t = raw.tile([P, 4 * D], BF16, align_bytes=64, name="pz_raw")
+            nc.sync.dma_start(out=t[:], in_=pz_h[n])
+            st["pz_raw", n] = t
+
+        def load_attn(n):
+            t = raw.tile([P, 4 * T], BF16, align_bytes=64, name="attn_raw")
+            nc.sync.dma_start(out=t[:], in_=attn_h[n])
+            st["attn_raw", n] = t
+
+        def load_x(b):
+            t = post.tile([P, 4, D], BF16, align_bytes=64, name="x_raw")
+            nc.sync.dma_start(out=t[:], in_=x_b[b])
+            st["x", b] = t
+
+        def attn_turn(n):
+            words = st["attn_raw", n][:].bitcast(F32)
+            g = grp.tile([P, T, 4], BF16, align_bytes=64, name="attn_g")
+            gw = g[:].rearrange("p c t -> p (c t)").bitcast(F32).rearrange("p (a r u) -> p a r u", a=4, u=2)
+            for h in range(2):
+                bank = ps_tr.tile([P, 2, 2, P], F32, name="tr")
+                for a in range(2):
+                    j = 2 * h + a
+                    for u in range(2):
+                        nc.tensor.transpose(bank[:, a, u, :], words[:, 256 * j + u : 256 * (j + 1) : 2], ident_f[:])
+                nc.scalar.copy(out=gw[:, 2 * h : 2 * h + 2], in_=bank[:].rearrange("p a u r -> p a r u"))
+            st["attn_g", n] = g
+
+        def pz_lay(n):
+            src = st["pz_raw", n][:].rearrange("p (j m t) -> p t m j", j=4, t=4)
+            g = grp.tile([P, 4, P, 4], BF16, align_bytes=64, name="pz_g")
+            if n in V_HEADS:
+                nc.vector.tensor_copy(out=g[:], in_=src)
+            elif n in S_HEADS:
+                for h in range(2):
+                    nc.scalar.copy(out=g[:, 2 * h : 2 * h + 2], in_=src[:, 2 * h : 2 * h + 2])
+            else:
+                for h in range(2):
+                    bank = ps_pz.tile([P, 2, P, 4], BF16, name="pzb")
+                    for a in range(2):
+                        nc.tensor.matmul(out=bank[:, a], lhsT=ident_b[:], rhs=src[:, 2 * h + a], start=True, stop=True)
+                    nc.scalar.copy(out=g[:, 2 * h : 2 * h + 2], in_=bank[:])
+            st["pz_g", n] = g
+
+        def quant(pool, name, flat):
+            c = pool.tile([P, 512], U32, align_bytes=64, name=name + "_c")
+            s = pool.tile([P, 512], U8, align_bytes=64, name=name + "_s")
+            nc.vector.quantize_mx(out=c[:].bitcast(FP8X4), scales=s[:], in_=flat)
+            return c, s
+
+        def q_attn(n):
+            st["attn_q", n] = quant(codes, "attn", st["attn_g", n][:].rearrange("p c t -> p (c t)"))
+
+        def q_pz(n):
+            st["pz_q", n] = quant(codes, "pz", st["pz_g", n][:].rearrange("p t m j -> p (t m j)"))
+
+        def q_cat(n):
+            st["cat_q", n] = quant(ccodes, "cat", st["cat_g", n][:].rearrange("p c t -> p (c t)"))
+
+        def stage1(n, j):
+            if j == 0:
+                st["cat_g", n] = grp.tile([P, T, 4], BF16, align_bytes=64, name="cat_g")
+            ac, asc = st["attn_q", n]
+            pc, psc = st["pz_q", n]
+            cols = slice(P * j, P * (j + 1))
+            bank = ps_cat.tile([P, 4, P], F32, name="catb")
+            for t in range(4):
+                ch = slice(P * t, P * (t + 1))
+                nc.tensor.matmul_mx(
+                    out=bank[:, t, :], lhsT=pc[:, ch].bitcast(FP8X4), lhsT_scale=psc[:, ch],
+                    rhs=ac[:, cols].bitcast(FP8X4), rhs_scale=asc[:, cols], start=True, stop=True)
+            nc.scalar.copy(out=st["cat_g", n][:, cols, :], in_=bank[:].rearrange("p t c -> p c t"))
+
+        def wo_part(q):
+            nc.scalar.copy(out=wo_wide[:, q, :], in_=wo_raw[:, q, :].bitcast(FP8))
+            words = wo_wide[:].rearrange("p q k -> p (q k)").bitcast(F32)
+            bank = ps_tr.tile([P, 2, 2, P], F32, name="tr")
+            for g in range(2):
+                for u in range(2):
+                    base = 512 * q + 256 * g
+                    nc.tensor.transpose(bank[:, g, u, :], words[:, base + u : base + 256 : 2], ident_f[:])
+            view = bank[:].rearrange("p g u r -> p (g u r)").bitcast(BF16).rearrange("p (g u r e) -> p g r u e", g=2, u=2, e=2)
+            for g in range(2):
+                nc.vector.tensor_tensor(
+                    out=wo_grp[:, g, P * q : P * (q + 1), :].rearrange("p r (u e) -> p r u e", e=2),
+                    in0=view[:, g],
+                    in1=wo_sc[:, g, :].rearrange("p (u e) -> p u e", e=2).unsqueeze(1).to_broadcast([P, P, 2, 2]),
+                    op=ALU.mult)
+
+        def wo_quant(g):
+            nc.vector.quantize_mx(out=wo_codes[:, g, :].bitcast(FP8X4), scales=wo_scales[:, g, :],
+                                  in_=wo_grp[:, g].rearrange("p c t -> p (c t)"))
+
+        def ymm(q):
+            b, h = divmod(q, 2)
+            banks = []
+            for a in range(2):
+                cols = slice(P * (2 * h + a), P * (2 * h + a + 1))
+                bank = ps_y.tile([P, D], F32, name="yb")
+                for m in range(2):
+                    cc, cs = st["cat_q", 2 * b + m]
+                    nc.tensor.matmul_mx(
+                        out=bank[:], lhsT=cc[:, cols].bitcast(FP8X4), lhsT_scale=cs[:, cols],
+                        rhs=wo_codes[:, m, :].bitcast(FP8X4), rhs_scale=wo_scales[:, m, :],
+                        start=(m == 0), stop=(m == 1))
+                banks.append(bank)
+            st["y", q] = banks
+
+        def xbias(q):
+            b, h = divmod(q, 2)
+            t = post.tile([P, 2, D], F32, align_bytes=64, name="xb")
+            nc.vector.tensor_tensor(out=t[:], in0=st["x", b][:, 2 * h : 2 * h + 2, :],
+                                    in1=bo_t[:].unsqueeze(1).to_broadcast([P, 2, D]), op=ALU.add)
+            st["xb", q] = t
+
+        def add_stats(q):
+            xb = st["xb", q]
+            h = post.tile([P, 2, D], F32, align_bytes=64, name="h")
+            sm = small.tile([P, 2], F32, name="sm")
+            for a in range(2):
+                nc.vector.scalar_tensor_tensor(out=h[:, a, :], in0=st["y", q][a][:], scalar=1.0, in1=xb[:, a, :],
+                                               op0=ALU.mult, op1=ALU.add, accum_out=sm[:, a : a + 1])
+            nm = small.tile([P, 2], F32, name="nm")
+            nc.scalar.activation(out=nm[:], in_=sm[:], func=ACT.Copy, scale=-1.0 / D)
+            ss = small.tile([P, 2], F32, name="ss")
+            for a in range(2):
+                junk = post.tile([P, D], BF16, align_bytes=64, name="junk")
+                nc.scalar.activation(out=junk[:], in_=h[:, a, :], func=ACT.Square, bias=nm[:, a : a + 1],
+                                     accum_out=ss[:, a : a + 1])
+            rs = small.tile([P, 2], F32, name="rs")
+            nc.scalar.activation(out=rs[:], in_=ss[:], func=ACT.Abs_reciprocal_sqrt, scale=1.0 / D, bias=1e-5)
+            st["h", q] = (h, nm, rs)
+
+        def finish(q):
+            b, half = divmod(q, 2)
+            h, nm, rs = st["h", q]
+            o = post.tile([P, 2, D], F32, align_bytes=64, name="o")
+            for a in range(2):
+                nc.vector.scalar_tensor_tensor(out=h[:, a, :], in0=h[:, a, :], scalar=nm[:, a : a + 1], in1=gamma_t[:],
+                                               op0=ALU.add, op1=ALU.mult)
+            for a in range(2):
+                nc.vector.scalar_tensor_tensor(out=o[:, a, :], in0=h[:, a, :], scalar=rs[:, a : a + 1], in1=beta_t[:],
+                                               op0=ALU.mult, op1=ALU.add)
+            nc.sync.dma_start(out=out_b[b, :, 2 * half : 2 * half + 2, :], in_=o[:])
+
+        load_pz(0)
+        load_attn(0)
+        load_pz(1)
+        load_attn(1)
+        nc.sync.dma_start(out=wo_raw[:], in_=Wo_bytes.rearrange("(q p) k -> p q k", p=P))
+        nc.sync.dma_start(out=wo_sc[:], in_=Wo_scale.rearrange("o (g p t) -> p (o g) t", p=P, t=4))
+        nc.sync.dma_start(out=bo_t[:], in_=bo.partition_broadcast(P))
+        load_x(0)
+        for n in range(2, LEAD):
+            load_pz(n)
+            load_attn(n)
+        nc.sync.dma_start(out=gamma_t[:], in_=gamma.partition_broadcast(P))
+        nc.sync.dma_start(out=beta_t[:], in_=beta.partition_broadcast(P))
+
+        for n in range(-1, N_HEADS + 3):
+            live = 0 <= n < N_HEADS
+            nxt = 0 <= n + 1 < N_HEADS
+            if 0 <= n and n + LEAD < N_HEADS:
+                load_pz(n + LEAD)
+                load_attn(n + LEAD)
+            if 0 <= n and n % 2 == 0 and n // 2 + 1 < B:
+                load_x(n // 2 + 1)
+            if 0 <= n - 1 < N_HEADS:
+                q_cat(n - 1)
+            if 0 <= n - 3 < N_HEADS:
+                finish(n - 3)
+            if live:
+                stage1(n, 0)
+                stage1(n, 1)
+            if nxt:
+                attn_turn(n + 1)
+            if live:
+                stage1(n, 2)
+                stage1(n, 3)
+            if n in (0, 1):
+                wo_part(2 * n)
+                wo_part(2 * n + 1)
+            if 0 <= n - 2 < N_HEADS:
+                ymm(n - 2)
+            if nxt:
+                pz_lay(n + 1)
+                q_attn(n + 1)
+            if 0 <= n - 2 < N_HEADS:
+                add_stats(n - 2)
+            if 0 <= n - 1 < N_HEADS:
+                xbias(n - 1)
+            if nxt:
+                q_pz(n + 1)
+            if n == 1:
+                wo_quant(0)
+                wo_quant(1)

@@ -17,8 +17,7 @@ ACT = mybir.ActivationFunctionType
 
 P = 128
 N_HEADS = B * HEADS
-V_HEADS = (0,)
-S_HEADS = (5, 9, 13)
+V_HEADS = (0, 1, 2, 8)
 LEAD = 4
 
 
@@ -33,14 +32,11 @@ def tile_softmaxattention_pb_t_kernel(tc, attn, pz, Wo_bytes, Wo_scale, bo, x, g
         post = ctx.enter_context(tc.tile_pool(name="post", bufs=3))
         small = ctx.enter_context(tc.tile_pool(name="small", bufs=4))
         ps_tr = ctx.enter_context(tc.psum_pool(name="ps_tr", bufs=2))
-        ps_cat = ctx.enter_context(tc.psum_pool(name="ps_cat", bufs=2))
+        ps_cat = ctx.enter_context(tc.psum_pool(name="ps_cat", bufs=4))
         ps_y = ctx.enter_context(tc.psum_pool(name="ps_y", bufs=2))
-        ps_pz = ctx.enter_context(tc.psum_pool(name="ps_pz", bufs=2))
 
         ident_f = const.tile([P, P], F32, align_bytes=64)
-        ident_b = const.tile([P, P], BF16, align_bytes=64)
         make_identity(nc, ident_f[:])
-        make_identity(nc, ident_b[:])
 
         wo_raw = const.tile([P, 4, HEADS * D], U8, align_bytes=64)
         wo_sc = const.tile([P, HEADS, 4], F32, align_bytes=64)
@@ -92,15 +88,9 @@ def tile_softmaxattention_pb_t_kernel(tc, attn, pz, Wo_bytes, Wo_scale, bo, x, g
             g = grp.tile([P, 4, P, 4], BF16, align_bytes=64, name="pz_g")
             if n in V_HEADS:
                 nc.vector.tensor_copy(out=g[:], in_=src)
-            elif n in S_HEADS:
-                for h in range(2):
-                    nc.scalar.copy(out=g[:, 2 * h : 2 * h + 2], in_=src[:, 2 * h : 2 * h + 2])
             else:
                 for h in range(2):
-                    bank = ps_pz.tile([P, 2, P, 4], BF16, name="pzb")
-                    for a in range(2):
-                        nc.tensor.matmul(out=bank[:, a], lhsT=ident_b[:], rhs=src[:, 2 * h + a], start=True, stop=True)
-                    nc.scalar.copy(out=g[:, 2 * h : 2 * h + 2], in_=bank[:])
+                    nc.scalar.copy(out=g[:, 2 * h : 2 * h + 2], in_=src[:, 2 * h : 2 * h + 2])
             st["pz_g", n] = g
 
         def quant(pool, name, flat):

@@ -17,7 +17,9 @@ ACT = mybir.ActivationFunctionType
 
 P = 128
 N_HEADS = B * HEADS
-V_HEADS = (0, 1, 2, 8)
+V_HEADS = (0, 1, 2, 3,)
+PE_HEADS = (4, 6, 8, 9, 10, 12, 14,)
+PE_PAIRS = (12, 13, 14, 15,)
 LEAD = 4
 
 
@@ -36,7 +38,12 @@ def tile_softmaxattention_pb_t_kernel(tc, attn, pz, Wo_bytes, Wo_scale, bo, x, g
         ps_y = ctx.enter_context(tc.psum_pool(name="ps_y", bufs=2))
 
         ident_f = const.tile([P, P], F32, align_bytes=64)
+        ident_b = const.tile([P, P], BF16, align_bytes=64)
         make_identity(nc, ident_f[:])
+        make_identity(nc, ident_b[:])
+        row0 = const.tile([P, P], BF16, align_bytes=64)
+        nc.gpsimd.memset(row0[:], 0.0)
+        nc.gpsimd.memset(row0[0:1, :], 1.0)
 
         wo_raw = const.tile([P, 4, HEADS * D], U8, align_bytes=64)
         wo_sc = const.tile([P, HEADS, 4], F32, align_bytes=64)
@@ -88,6 +95,12 @@ def tile_softmaxattention_pb_t_kernel(tc, attn, pz, Wo_bytes, Wo_scale, bo, x, g
             g = grp.tile([P, 4, P, 4], BF16, align_bytes=64, name="pz_g")
             if n in V_HEADS:
                 nc.vector.tensor_copy(out=g[:], in_=src)
+            elif n in PE_HEADS:
+                for h in range(2):
+                    bank = ps_tr.tile([P, 2, P, 4], BF16, name="tr")
+                    for a in range(2):
+                        nc.tensor.matmul(out=bank[:, a], lhsT=ident_b[:], rhs=src[:, 2 * h + a], start=True, stop=True)
+                    nc.scalar.copy(out=g[:, 2 * h : 2 * h + 2], in_=bank[:])
             else:
                 for h in range(2):
                     nc.scalar.copy(out=g[:, 2 * h : 2 * h + 2], in_=src[:, 2 * h : 2 * h + 2])
@@ -122,8 +135,10 @@ def tile_softmaxattention_pb_t_kernel(tc, attn, pz, Wo_bytes, Wo_scale, bo, x, g
                     rhs=ac[:, cols].bitcast(FP8X4), rhs_scale=asc[:, cols], start=True, stop=True)
             nc.scalar.copy(out=st["cat_g", n][:, cols, :], in_=bank[:].rearrange("p t c -> p c t"))
 
-        def wo_part(q):
+        def wo_widen(q):
             nc.scalar.copy(out=wo_wide[:, q, :], in_=wo_raw[:, q, :].bitcast(FP8))
+
+        def wo_turn(q):
             words = wo_wide[:].rearrange("p q k -> p (q k)").bitcast(F32)
             bank = ps_tr.tile([P, 2, 2, P], F32, name="tr")
             for g in range(2):
@@ -160,11 +175,18 @@ def tile_softmaxattention_pb_t_kernel(tc, attn, pz, Wo_bytes, Wo_scale, bo, x, g
         def xbias(q):
             b, h = divmod(q, 2)
             t = post.tile([P, 2, D], F32, align_bytes=64, name="xb")
+            st["xb", q] = t
+            if q in PE_PAIRS:
+                for a in range(2):
+                    bank = ps_tr.tile([P, D], F32, name="tr")
+                    nc.tensor.matmul(out=bank[:], lhsT=ident_b[:], rhs=st["x", b][:, 2 * h + a, :], start=True, stop=False)
+                    nc.tensor.matmul(out=bank[:], lhsT=row0[:], rhs=bo_t[:], start=False, stop=True)
+                    nc.scalar.copy(out=t[:, a, :], in_=bank[:])
+                return
             nc.vector.tensor_tensor(out=t[:], in0=st["x", b][:, 2 * h : 2 * h + 2, :],
                                     in1=bo_t[:].unsqueeze(1).to_broadcast([P, 2, D]), op=ALU.add)
-            st["xb", q] = t
 
-        def add_stats(q):
+        def add(q):
             xb = st["xb", q]
             h = post.tile([P, 2, D], F32, align_bytes=64, name="h")
             sm = small.tile([P, 2], F32, name="sm")
@@ -172,76 +194,368 @@ def tile_softmaxattention_pb_t_kernel(tc, attn, pz, Wo_bytes, Wo_scale, bo, x, g
                 nc.vector.scalar_tensor_tensor(out=h[:, a, :], in0=st["y", q][a][:], scalar=1.0, in1=xb[:, a, :],
                                                op0=ALU.mult, op1=ALU.add, accum_out=sm[:, a : a + 1])
             nm = small.tile([P, 2], F32, name="nm")
-            nc.scalar.activation(out=nm[:], in_=sm[:], func=ACT.Copy, scale=-1.0 / D)
+            nc.gpsimd.tensor_scalar(out=nm[:], in0=sm[:], scalar1=-1.0 / D, scalar2=0.0, op0=ALU.mult, op1=ALU.add)
+            st["h", q] = (h, nm)
+
+        def squares(q):
+            h, nm = st["h", q]
             ss = small.tile([P, 2], F32, name="ss")
             for a in range(2):
                 junk = post.tile([P, D], BF16, align_bytes=64, name="junk")
                 nc.scalar.activation(out=junk[:], in_=h[:, a, :], func=ACT.Square, bias=nm[:, a : a + 1],
                                      accum_out=ss[:, a : a + 1])
-            rs = small.tile([P, 2], F32, name="rs")
-            nc.scalar.activation(out=rs[:], in_=ss[:], func=ACT.Abs_reciprocal_sqrt, scale=1.0 / D, bias=1e-5)
-            st["h", q] = (h, nm, rs)
+            st["ss", q] = ss
 
-        def finish(q):
-            b, half = divmod(q, 2)
-            h, nm, rs = st["h", q]
-            o = post.tile([P, 2, D], F32, align_bytes=64, name="o")
+        def rstd(q):
+            rs = small.tile([P, 2], F32, name="rs")
+            nc.scalar.activation(out=rs[:], in_=st["ss", q][:], func=ACT.Abs_reciprocal_sqrt, scale=1.0 / D, bias=1e-5)
+            st["rs", q] = rs
+
+        def center(q):
+            h, nm = st["h", q]
             for a in range(2):
                 nc.vector.scalar_tensor_tensor(out=h[:, a, :], in0=h[:, a, :], scalar=nm[:, a : a + 1], in1=gamma_t[:],
                                                op0=ALU.add, op1=ALU.mult)
+
+        def finish(q):
+            b, half = divmod(q, 2)
+            h, nm = st["h", q]
+            rs = st["rs", q]
+            o = post.tile([P, 2, D], F32, align_bytes=64, name="o")
             for a in range(2):
                 nc.vector.scalar_tensor_tensor(out=o[:, a, :], in0=h[:, a, :], scalar=rs[:, a : a + 1], in1=beta_t[:],
                                                op0=ALU.mult, op1=ALU.add)
-            nc.sync.dma_start(out=out_b[b, :, 2 * half : 2 * half + 2, :], in_=o[:])
+            st["o", q] = o
 
-        load_pz(0)
+        def store(q):
+            b, half = divmod(q, 2)
+            nc.sync.dma_start(out=out_b[b, :, 2 * half : 2 * half + 2, :], in_=st["o", q][:])
+
+        ctx.enter_context(tc.manual_schedule())
         load_attn(0)
-        load_pz(1)
-        load_attn(1)
         nc.sync.dma_start(out=wo_raw[:], in_=Wo_bytes.rearrange("(q p) k -> p q k", p=P))
         nc.sync.dma_start(out=wo_sc[:], in_=Wo_scale.rearrange("o (g p t) -> p (o g) t", p=P, t=4))
-        nc.sync.dma_start(out=bo_t[:], in_=bo.partition_broadcast(P))
+        load_pz(0)
+        load_attn(1)
+        load_pz(1)
+        load_attn(2)
+        load_pz(2)
         load_x(0)
-        for n in range(2, LEAD):
-            load_pz(n)
-            load_attn(n)
+        nc.sync.dma_start(out=bo_t[:], in_=bo.partition_broadcast(P))
+        load_attn(3)
+        load_pz(3)
         nc.sync.dma_start(out=gamma_t[:], in_=gamma.partition_broadcast(P))
         nc.sync.dma_start(out=beta_t[:], in_=beta.partition_broadcast(P))
-
-        for n in range(-1, N_HEADS + 3):
-            live = 0 <= n < N_HEADS
-            nxt = 0 <= n + 1 < N_HEADS
-            if 0 <= n and n + LEAD < N_HEADS:
-                load_pz(n + LEAD)
-                load_attn(n + LEAD)
-            if 0 <= n and n % 2 == 0 and n // 2 + 1 < B:
-                load_x(n // 2 + 1)
-            if 0 <= n - 1 < N_HEADS:
-                q_cat(n - 1)
-            if 0 <= n - 3 < N_HEADS:
-                finish(n - 3)
-            if live:
-                stage1(n, 0)
-                stage1(n, 1)
-            if nxt:
-                attn_turn(n + 1)
-            if live:
-                stage1(n, 2)
-                stage1(n, 3)
-            if n in (0, 1):
-                wo_part(2 * n)
-                wo_part(2 * n + 1)
-            if 0 <= n - 2 < N_HEADS:
-                ymm(n - 2)
-            if nxt:
-                pz_lay(n + 1)
-                q_attn(n + 1)
-            if 0 <= n - 2 < N_HEADS:
-                add_stats(n - 2)
-            if 0 <= n - 1 < N_HEADS:
-                xbias(n - 1)
-            if nxt:
-                q_pz(n + 1)
-            if n == 1:
-                wo_quant(0)
-                wo_quant(1)
+        load_x(1)
+        attn_turn(0)
+        pz_lay(0)
+        wo_widen(0)
+        q_attn(0)
+        wo_widen(1)
+        attn_turn(1)
+        pz_lay(1)
+        q_pz(0)
+        wo_widen(2)
+        wo_widen(3)
+        wo_turn(0)
+        wo_turn(1)
+        q_attn(1)
+        q_pz(1)
+        stage1(0, 0)
+        stage1(0, 1)
+        stage1(0, 2)
+        stage1(0, 3)
+        load_attn(4)
+        load_pz(4)
+        attn_turn(2)
+        pz_lay(2)
+        wo_turn(2)
+        wo_turn(3)
+        q_attn(2)
+        q_cat(0)
+        xbias(0)
+        q_pz(2)
+        wo_quant(0)
+        wo_quant(1)
+        stage1(1, 0)
+        stage1(1, 1)
+        stage1(1, 2)
+        stage1(1, 3)
+        load_attn(5)
+        load_pz(5)
+        attn_turn(3)
+        pz_lay(3)
+        load_attn(6)
+        load_pz(6)
+        load_x(2)
+        q_cat(1)
+        stage1(2, 0)
+        stage1(2, 1)
+        stage1(2, 2)
+        stage1(2, 3)
+        q_attn(3)
+        attn_turn(4)
+        ymm(0)
+        q_pz(3)
+        pz_lay(4)
+        load_attn(7)
+        load_pz(7)
+        q_cat(2)
+        stage1(3, 0)
+        stage1(3, 1)
+        stage1(3, 2)
+        stage1(3, 3)
+        add(0)
+        q_attn(4)
+        attn_turn(5)
+        ymm(1)
+        squares(0)
+        q_pz(4)
+        pz_lay(5)
+        xbias(1)
+        load_attn(8)
+        load_pz(8)
+        load_x(3)
+        q_cat(3)
+        stage1(4, 0)
+        rstd(0)
+        stage1(4, 1)
+        stage1(4, 2)
+        stage1(4, 3)
+        add(1)
+        q_attn(5)
+        center(0)
+        attn_turn(6)
+        ymm(2)
+        squares(1)
+        q_pz(5)
+        finish(0)
+        pz_lay(6)
+        xbias(2)
+        load_attn(9)
+        load_pz(9)
+        store(0)
+        q_cat(4)
+        stage1(5, 0)
+        rstd(1)
+        stage1(5, 1)
+        stage1(5, 2)
+        stage1(5, 3)
+        add(2)
+        q_attn(6)
+        center(1)
+        attn_turn(7)
+        ymm(3)
+        squares(2)
+        q_pz(6)
+        finish(1)
+        pz_lay(7)
+        xbias(3)
+        load_attn(10)
+        load_pz(10)
+        load_x(4)
+        store(1)
+        q_cat(5)
+        stage1(6, 0)
+        rstd(2)
+        stage1(6, 1)
+        stage1(6, 2)
+        stage1(6, 3)
+        add(3)
+        q_attn(7)
+        center(2)
+        attn_turn(8)
+        ymm(4)
+        squares(3)
+        q_pz(7)
+        finish(2)
+        pz_lay(8)
+        xbias(4)
+        load_attn(11)
+        load_pz(11)
+        store(2)
+        q_cat(6)
+        stage1(7, 0)
+        rstd(3)
+        stage1(7, 1)
+        stage1(7, 2)
+        stage1(7, 3)
+        add(4)
+        q_attn(8)
+        center(3)
+        attn_turn(9)
+        ymm(5)
+        squares(4)
+        q_pz(8)
+        finish(3)
+        pz_lay(9)
+        xbias(5)
+        load_attn(12)
+        load_pz(12)
+        load_x(5)
+        store(3)
+        q_cat(7)
+        stage1(8, 0)
+        rstd(4)
+        stage1(8, 1)
+        stage1(8, 2)
+        stage1(8, 3)
+        add(5)
+        q_attn(9)
+        center(4)
+        attn_turn(10)
+        ymm(6)
+        squares(5)
+        q_pz(9)
+        finish(4)
+        pz_lay(10)
+        xbias(6)
+        load_attn(13)
+        load_pz(13)
+        store(4)
+        q_cat(8)
+        stage1(9, 0)
+        rstd(5)
+        stage1(9, 1)
+        stage1(9, 2)
+        stage1(9, 3)
+        add(6)
+        q_attn(10)
+        center(5)
+        attn_turn(11)
+        ymm(7)
+        squares(6)
+        q_pz(10)
+        finish(5)
+        pz_lay(11)
+        xbias(7)
+        load_attn(14)
+        load_pz(14)
+        load_x(6)
+        store(5)
+        q_cat(9)
+        stage1(10, 0)
+        rstd(6)
+        stage1(10, 1)
+        stage1(10, 2)
+        stage1(10, 3)
+        add(7)
+        q_attn(11)
+        center(6)
+        attn_turn(12)
+        ymm(8)
+        squares(7)
+        q_pz(11)
+        finish(6)
+        pz_lay(12)
+        xbias(8)
+        load_attn(15)
+        load_pz(15)
+        store(6)
+        q_cat(10)
+        stage1(11, 0)
+        rstd(7)
+        stage1(11, 1)
+        stage1(11, 2)
+        stage1(11, 3)
+        add(8)
+        q_attn(12)
+        center(7)
+        attn_turn(13)
+        ymm(9)
+        squares(8)
+        q_pz(12)
+        finish(7)
+        pz_lay(13)
+        xbias(9)
+        load_x(7)
+        store(7)
+        q_cat(11)
+        stage1(12, 0)
+        rstd(8)
+        stage1(12, 1)
+        stage1(12, 2)
+        stage1(12, 3)
+        add(9)
+        q_attn(13)
+        center(8)
+        attn_turn(14)
+        ymm(10)
+        squares(9)
+        q_pz(13)
+        finish(8)
+        pz_lay(14)
+        xbias(10)
+        store(8)
+        q_cat(12)
+        stage1(13, 0)
+        rstd(9)
+        stage1(13, 1)
+        stage1(13, 2)
+        stage1(13, 3)
+        add(10)
+        q_attn(14)
+        center(9)
+        attn_turn(15)
+        ymm(11)
+        squares(10)
+        q_pz(14)
+        finish(9)
+        pz_lay(15)
+        xbias(11)
+        store(9)
+        q_cat(13)
+        stage1(14, 0)
+        rstd(10)
+        stage1(14, 1)
+        stage1(14, 2)
+        stage1(14, 3)
+        add(11)
+        q_attn(15)
+        center(10)
+        ymm(12)
+        squares(11)
+        q_pz(15)
+        finish(10)
+        xbias(12)
+        store(10)
+        q_cat(14)
+        stage1(15, 0)
+        rstd(11)
+        stage1(15, 1)
+        stage1(15, 2)
+        stage1(15, 3)
+        add(12)
+        center(11)
+        ymm(13)
+        squares(12)
+        finish(11)
+        xbias(13)
+        store(11)
+        q_cat(15)
+        rstd(12)
+        add(13)
+        center(12)
+        ymm(14)
+        squares(13)
+        finish(12)
+        xbias(14)
+        store(12)
+        rstd(13)
+        add(14)
+        center(13)
+        ymm(15)
+        squares(14)
+        finish(13)
+        xbias(15)
+        store(13)
+        rstd(14)
+        add(15)
+        center(14)
+        squares(15)
+        finish(14)
+        store(14)
+        rstd(15)
+        center(15)
+        finish(15)
+        store(15)

@@ -17,9 +17,9 @@ ACT = mybir.ActivationFunctionType
 
 P = 128
 N_HEADS = B * HEADS
-V_HEADS = (0, 1, 2, 3,)
-PE_HEADS = (4, 6, 8, 9, 10, 12, 14,)
-PE_PAIRS = (12, 13, 14, 15,)
+V_HEADS = (0, 1, 2, 3, 4, 5, 6, 7, 8, 9, 10, 11, 12, 13, 14, 15,)
+PE_HEADS = ()
+PE_PAIRS = ()
 LEAD = 4
 
 

@@ -17,9 +17,7 @@ ACT = mybir.ActivationFunctionType
 
 P = 128
 N_HEADS = B * HEADS
-V_HEADS = (0, 1, 2, 3, 4, 5, 6, 7, 8, 9, 10, 11, 12, 13, 14, 15,)
-PE_HEADS = ()
-PE_PAIRS = ()
+PE_PAIRS = (4, 5, 6, 7, 8, 9, 10, 11, 12, 13, 14, 15)
 LEAD = 4
 
 
@@ -46,8 +44,9 @@ def tile_softmaxattention_pb_t_kernel(tc, attn, pz, Wo_bytes, Wo_scale, bo, x, g
         nc.gpsimd.memset(row0[0:1, :], 1.0)
 
         wo_raw = const.tile([P, 4, HEADS * D], U8, align_bytes=64)
-        wo_sc = const.tile([P, HEADS, 4], F32, align_bytes=64)
-        wo_wide = const.tile([P, 4, HEADS * D], BF16, align_bytes=64)
+        wo_sc = const.tile([P, HEADS * D], F32, align_bytes=64)
+        wo_w = const.tile([P, 4, HEADS * D], BF16, align_bytes=64)
+        wo_p = const.tile([P, 4, HEADS, 4, P], BF16, align_bytes=64)
         wo_grp = const.tile([P, HEADS, D, 4], BF16, align_bytes=64)
         wo_codes = const.tile([P, HEADS, D], U32, align_bytes=64)
         wo_scales = const.tile([P, HEADS, D], U8, align_bytes=64)
@@ -79,8 +78,9 @@ def tile_softmaxattention_pb_t_kernel(tc, attn, pz, Wo_bytes, Wo_scale, bo, x, g
 
         def attn_turn(n):
             words = st["attn_raw", n][:].bitcast(F32)
-            g = grp.tile([P, T, 4], BF16, align_bytes=64, name="attn_g")
-            gw = g[:].rearrange("p c t -> p (c t)").bitcast(F32).rearrange("p (a r u) -> p a r u", a=4, u=2)
+            both = grp.tile([P, 2, 4 * D], BF16, align_bytes=64, name="in_g")
+            st["in_g", n] = both
+            gw = both[:, 0, :].bitcast(F32).rearrange("p (a r u) -> p a r u", a=4, u=2)
             for h in range(2):
                 bank = ps_tr.tile([P, 2, 2, P], F32, name="tr")
                 for a in range(2):
@@ -88,70 +88,53 @@ def tile_softmaxattention_pb_t_kernel(tc, attn, pz, Wo_bytes, Wo_scale, bo, x, g
                     for u in range(2):
                         nc.tensor.transpose(bank[:, a, u, :], words[:, 256 * j + u : 256 * (j + 1) : 2], ident_f[:])
                 nc.scalar.copy(out=gw[:, 2 * h : 2 * h + 2], in_=bank[:].rearrange("p a u r -> p a r u"))
-            st["attn_g", n] = g
 
         def pz_lay(n):
-            src = st["pz_raw", n][:].rearrange("p (j m t) -> p t m j", j=4, t=4)
-            g = grp.tile([P, 4, P, 4], BF16, align_bytes=64, name="pz_g")
-            if n in V_HEADS:
-                nc.vector.tensor_copy(out=g[:], in_=src)
-            elif n in PE_HEADS:
-                for h in range(2):
-                    bank = ps_tr.tile([P, 2, P, 4], BF16, name="tr")
-                    for a in range(2):
-                        nc.tensor.matmul(out=bank[:, a], lhsT=ident_b[:], rhs=src[:, 2 * h + a], start=True, stop=True)
-                    nc.scalar.copy(out=g[:, 2 * h : 2 * h + 2], in_=bank[:])
-            else:
-                for h in range(2):
-                    nc.scalar.copy(out=g[:, 2 * h : 2 * h + 2], in_=src[:, 2 * h : 2 * h + 2])
-            st["pz_g", n] = g
+            src = st["pz_raw", n][:].rearrange("p (j b t i) -> p b t j i", j=4, b=32, t=4)
+            dst = st["in_g", n][:, 1, :].rearrange("p (t b i j) -> p b t j i", t=4, b=32, i=4)
+            nc.vector.tensor_copy(out=dst, in_=src)
 
-        def quant(pool, name, flat):
-            c = pool.tile([P, 512], U32, align_bytes=64, name=name + "_c")
-            s = pool.tile([P, 512], U8, align_bytes=64, name=name + "_s")
-            nc.vector.quantize_mx(out=c[:].bitcast(FP8X4), scales=s[:], in_=flat)
-            return c, s
-
-        def q_attn(n):
-            st["attn_q", n] = quant(codes, "attn", st["attn_g", n][:].rearrange("p c t -> p (c t)"))
-
-        def q_pz(n):
-            st["pz_q", n] = quant(codes, "pz", st["pz_g", n][:].rearrange("p t m j -> p (t m j)"))
+        def q_in(n):
+            c = codes.tile([P, 2, 512], U32, align_bytes=64, name="in_c")
+            s = codes.tile([P, 2, 512], U8, align_bytes=64, name="in_s")
+            nc.vector.quantize_mx(out=c[:].rearrange("p a w -> p (a w)").bitcast(FP8X4), scales=s[:].rearrange("p a w -> p (a w)"),
+                                  in_=st["in_g", n][:].rearrange("p a w -> p (a w)"))
+            st["in_q", n] = (c, s)
 
         def q_cat(n):
-            st["cat_q", n] = quant(ccodes, "cat", st["cat_g", n][:].rearrange("p c t -> p (c t)"))
+            c = ccodes.tile([P, 512], U32, align_bytes=64, name="cat_c")
+            s = ccodes.tile([P, 512], U8, align_bytes=64, name="cat_s")
+            nc.vector.quantize_mx(out=c[:].bitcast(FP8X4), scales=s[:], in_=st["cat_g", n][:].rearrange("p c t -> p (c t)"))
+            st["cat_q", n] = (c, s)
 
         def stage1(n, j):
             if j == 0:
                 st["cat_g", n] = grp.tile([P, T, 4], BF16, align_bytes=64, name="cat_g")
-            ac, asc = st["attn_q", n]
-            pc, psc = st["pz_q", n]
+            ic, isc = st["in_q", n]
             cols = slice(P * j, P * (j + 1))
             bank = ps_cat.tile([P, 4, P], F32, name="catb")
             for t in range(4):
                 ch = slice(P * t, P * (t + 1))
                 nc.tensor.matmul_mx(
-                    out=bank[:, t, :], lhsT=pc[:, ch].bitcast(FP8X4), lhsT_scale=psc[:, ch],
-                    rhs=ac[:, cols].bitcast(FP8X4), rhs_scale=asc[:, cols], start=True, stop=True)
+                    out=bank[:, t, :], lhsT=ic[:, 1, ch].bitcast(FP8X4), lhsT_scale=isc[:, 1, ch],
+                    rhs=ic[:, 0, cols].bitcast(FP8X4), rhs_scale=isc[:, 0, cols], start=True, stop=True)
             nc.scalar.copy(out=st["cat_g", n][:, cols, :], in_=bank[:].rearrange("p t c -> p c t"))
 
-        def wo_widen(q):
-            nc.scalar.copy(out=wo_wide[:, q, :], in_=wo_raw[:, q, :].bitcast(FP8))
+        def wo_scale(q):
+            nc.vector.tensor_tensor(out=wo_w[:, q, :], in0=wo_raw[:, q, :].bitcast(FP8), in1=wo_sc[:], op=ALU.mult)
+
+        def wo_order(q):
+            for g in range(HEADS):
+                nc.scalar.copy(
+                    out=wo_p[:, q, g].rearrange("p t (b i) -> p t b i", b=32),
+                    in_=wo_w[:, q, D * g : D * (g + 1)].rearrange("p (b t i) -> p t b i", b=32, t=4))
 
         def wo_turn(q):
-            words = wo_wide[:].rearrange("p q k -> p (q k)").bitcast(F32)
-            bank = ps_tr.tile([P, 2, 2, P], F32, name="tr")
-            for g in range(2):
-                for u in range(2):
-                    base = 512 * q + 256 * g
-                    nc.tensor.transpose(bank[:, g, u, :], words[:, base + u : base + 256 : 2], ident_f[:])
-            view = bank[:].rearrange("p g u r -> p (g u r)").bitcast(BF16).rearrange("p (g u r e) -> p g r u e", g=2, u=2, e=2)
-            for g in range(2):
-                nc.vector.tensor_tensor(
-                    out=wo_grp[:, g, P * q : P * (q + 1), :].rearrange("p r (u e) -> p r u e", e=2),
-                    in0=view[:, g],
-                    in1=wo_sc[:, g, :].rearrange("p (u e) -> p u e", e=2).unsqueeze(1).to_broadcast([P, P, 2, 2]),
-                    op=ALU.mult)
+            bank = ps_tr.tile([P, HEADS, 4, P], BF16, name="tr")
+            for g in range(HEADS):
+                for t in range(4):
+                    nc.tensor.transpose(bank[:, g, t, :], wo_p[:, q, g, t, :], ident_b[:])
+            nc.scalar.copy(out=wo_grp[:, :, P * q : P * (q + 1), :], in_=bank[:].rearrange("p g t o -> p g o t"))
 
         def wo_quant(g):
             nc.vector.quantize_mx(out=wo_codes[:, g, :].bitcast(FP8X4), scales=wo_scales[:, g, :],
@@ -193,9 +176,13 @@ def tile_softmaxattention_pb_t_kernel(tc, attn, pz, Wo_bytes, Wo_scale, bo, x, g
             for a in range(2):
                 nc.vector.scalar_tensor_tensor(out=h[:, a, :], in0=st["y", q][a][:], scalar=1.0, in1=xb[:, a, :],
                                                op0=ALU.mult, op1=ALU.add, accum_out=sm[:, a : a + 1])
+            st["sm", q] = sm
+            st["hh", q] = h
+
+        def negmean(q):
             nm = small.tile([P, 2], F32, name="nm")
-            nc.gpsimd.tensor_scalar(out=nm[:], in0=sm[:], scalar1=-1.0 / D, scalar2=0.0, op0=ALU.mult, op1=ALU.add)
-            st["h", q] = (h, nm)
+            nc.scalar.activation(out=nm[:], in_=st["sm", q][:], func=ACT.Copy, scale=-1.0 / D)
+            st["h", q] = (st["hh", q], nm)
 
         def squares(q):
             h, nm = st["h", q]
@@ -229,17 +216,21 @@ def tile_softmaxattention_pb_t_kernel(tc, attn, pz, Wo_bytes, Wo_scale, bo, x, g
 
         def store(q):
             b, half = divmod(q, 2)
-            nc.sync.dma_start(out=out_b[b, :, 2 * half : 2 * half + 2, :], in_=st["o", q][:])
+            if q < N_HEADS - 1:
+                nc.sync.dma_start(out=out_b[b, :, 2 * half : 2 * half + 2, :], in_=st["o", q][:])
+            else:
+                for a in range(2):
+                    nc.sync.dma_start(out=out_b[b, :, 2 * half + a, :], in_=st["o", q][:, a, :])
 
         ctx.enter_context(tc.manual_schedule())
         load_attn(0)
-        nc.sync.dma_start(out=wo_raw[:], in_=Wo_bytes.rearrange("(q p) k -> p q k", p=P))
-        nc.sync.dma_start(out=wo_sc[:], in_=Wo_scale.rearrange("o (g p t) -> p (o g) t", p=P, t=4))
         load_pz(0)
         load_attn(1)
         load_pz(1)
         load_attn(2)
         load_pz(2)
+        nc.sync.dma_start(out=wo_sc[:], in_=Wo_scale.rearrange("o k -> (o k)").partition_broadcast(P))
+        nc.sync.dma_start(out=wo_raw[:], in_=Wo_bytes.rearrange("(q p) k -> p q k", p=P))
         load_x(0)
         nc.sync.dma_start(out=bo_t[:], in_=bo.partition_broadcast(P))
         load_attn(3)
@@ -247,56 +238,56 @@ def tile_softmaxattention_pb_t_kernel(tc, attn, pz, Wo_bytes, Wo_scale, bo, x, g
         nc.sync.dma_start(out=gamma_t[:], in_=gamma.partition_broadcast(P))
         nc.sync.dma_start(out=beta_t[:], in_=beta.partition_broadcast(P))
         load_x(1)
+        load_attn(4)
+        load_pz(4)
+        load_attn(5)
+        load_pz(5)
+        load_attn(6)
+        load_pz(6)
         attn_turn(0)
         pz_lay(0)
-        wo_widen(0)
-        q_attn(0)
-        wo_widen(1)
         attn_turn(1)
+        q_in(0)
         pz_lay(1)
-        q_pz(0)
-        wo_widen(2)
-        wo_widen(3)
-        wo_turn(0)
-        wo_turn(1)
-        q_attn(1)
-        q_pz(1)
+        q_in(1)
         stage1(0, 0)
         stage1(0, 1)
         stage1(0, 2)
         stage1(0, 3)
-        load_attn(4)
-        load_pz(4)
+        wo_scale(0)
+        wo_scale(1)
+        wo_scale(2)
+        wo_scale(3)
         attn_turn(2)
         pz_lay(2)
-        wo_turn(2)
-        wo_turn(3)
-        q_attn(2)
-        q_cat(0)
-        xbias(0)
-        q_pz(2)
-        wo_quant(0)
-        wo_quant(1)
         stage1(1, 0)
         stage1(1, 1)
+        wo_order(0)
+        wo_order(1)
+        wo_order(2)
+        wo_order(3)
         stage1(1, 2)
         stage1(1, 3)
-        load_attn(5)
-        load_pz(5)
+        q_in(2)
+        wo_turn(0)
+        wo_turn(1)
+        wo_turn(2)
+        wo_turn(3)
         attn_turn(3)
+        xbias(0)
         pz_lay(3)
-        load_attn(6)
-        load_pz(6)
+        q_cat(0)
+        wo_quant(0)
+        wo_quant(1)
         load_x(2)
         q_cat(1)
         stage1(2, 0)
         stage1(2, 1)
         stage1(2, 2)
         stage1(2, 3)
-        q_attn(3)
+        q_in(3)
         attn_turn(4)
         ymm(0)
-        q_pz(3)
         pz_lay(4)
         load_attn(7)
         load_pz(7)
@@ -306,11 +297,11 @@ def tile_softmaxattention_pb_t_kernel(tc, attn, pz, Wo_bytes, Wo_scale, bo, x, g
         stage1(3, 2)
         stage1(3, 3)
         add(0)
-        q_attn(4)
+        q_in(4)
+        negmean(0)
         attn_turn(5)
         ymm(1)
         squares(0)
-        q_pz(4)
         pz_lay(5)
         xbias(1)
         load_attn(8)
@@ -323,12 +314,12 @@ def tile_softmaxattention_pb_t_kernel(tc, attn, pz, Wo_bytes, Wo_scale, bo, x, g
         stage1(4, 2)
         stage1(4, 3)
         add(1)
-        q_attn(5)
+        q_in(5)
         center(0)
+        negmean(1)
         attn_turn(6)
         ymm(2)
         squares(1)
-        q_pz(5)
         finish(0)
         pz_lay(6)
         xbias(2)
@@ -342,12 +333,12 @@ def tile_softmaxattention_pb_t_kernel(tc, attn, pz, Wo_bytes, Wo_scale, bo, x, g
         stage1(5, 2)
         stage1(5, 3)
         add(2)
-        q_attn(6)
+        q_in(6)
         center(1)
+        negmean(2)
         attn_turn(7)
         ymm(3)
         squares(2)
-        q_pz(6)
         finish(1)
         pz_lay(7)
         xbias(3)
@@ -362,12 +353,12 @@ def tile_softmaxattention_pb_t_kernel(tc, attn, pz, Wo_bytes, Wo_scale, bo, x, g
         stage1(6, 2)
         stage1(6, 3)
         add(3)
-        q_attn(7)
+        q_in(7)
         center(2)
+        negmean(3)
         attn_turn(8)
         ymm(4)
         squares(3)
-        q_pz(7)
         finish(2)
         pz_lay(8)
         xbias(4)
@@ -381,12 +372,12 @@ def tile_softmaxattention_pb_t_kernel(tc, attn, pz, Wo_bytes, Wo_scale, bo, x, g
         stage1(7, 2)
         stage1(7, 3)
         add(4)
-        q_attn(8)
+        q_in(8)
         center(3)
+        negmean(4)
         attn_turn(9)
         ymm(5)
         squares(4)
-        q_pz(8)
         finish(3)
         pz_lay(9)
         xbias(5)
@@ -401,12 +392,12 @@ def tile_softmaxattention_pb_t_kernel(tc, attn, pz, Wo_bytes, Wo_scale, bo, x, g
         stage1(8, 2)
         stage1(8, 3)
         add(5)
-        q_attn(9)
+        q_in(9)
         center(4)
+        negmean(5)
         attn_turn(10)
         ymm(6)
         squares(5)
-        q_pz(9)
         finish(4)
         pz_lay(10)
         xbias(6)
@@ -420,12 +411,12 @@ def tile_softmaxattention_pb_t_kernel(tc, attn, pz, Wo_bytes, Wo_scale, bo, x, g
         stage1(9, 2)
         stage1(9, 3)
         add(6)
-        q_attn(10)
+        q_in(10)
         center(5)
+        negmean(6)
         attn_turn(11)
         ymm(7)
         squares(6)
-        q_pz(10)
         finish(5)
         pz_lay(11)
         xbias(7)
@@ -440,12 +431,12 @@ def tile_softmaxattention_pb_t_kernel(tc, attn, pz, Wo_bytes, Wo_scale, bo, x, g
         stage1(10, 2)
         stage1(10, 3)
         add(7)
-        q_attn(11)
+        q_in(11)
         center(6)
+        negmean(7)
         attn_turn(12)
         ymm(8)
         squares(7)
-        q_pz(11)
         finish(6)
         pz_lay(12)
         xbias(8)
@@ -459,12 +450,12 @@ def tile_softmaxattention_pb_t_kernel(tc, attn, pz, Wo_bytes, Wo_scale, bo, x, g
         stage1(11, 2)
         stage1(11, 3)
         add(8)
-        q_attn(12)
+        q_in(12)
         center(7)
+        negmean(8)
         attn_turn(13)
         ymm(9)
         squares(8)
-        q_pz(12)
         finish(7)
         pz_lay(13)
         xbias(9)
@@ -477,12 +468,12 @@ def tile_softmaxattention_pb_t_kernel(tc, attn, pz, Wo_bytes, Wo_scale, bo, x, g
         stage1(12, 2)
         stage1(12, 3)
         add(9)
-        q_attn(13)
+        q_in(13)
         center(8)
+        negmean(9)
         attn_turn(14)
         ymm(10)
         squares(9)
-        q_pz(13)
         finish(8)
         pz_lay(14)
         xbias(10)
@@ -494,12 +485,12 @@ def tile_softmaxattention_pb_t_kernel(tc, attn, pz, Wo_bytes, Wo_scale, bo, x, g
         stage1(13, 2)
         stage1(13, 3)
         add(10)
-        q_attn(14)
+        q_in(14)
         center(9)
+        negmean(10)
         attn_turn(15)
         ymm(11)
         squares(10)
-        q_pz(14)
         finish(9)
         pz_lay(15)
         xbias(11)
@@ -511,11 +502,11 @@ def tile_softmaxattention_pb_t_kernel(tc, attn, pz, Wo_bytes, Wo_scale, bo, x, g
         stage1(14, 2)
         stage1(14, 3)
         add(11)
-        q_attn(15)
+        q_in(15)
         center(10)
+        negmean(11)
         ymm(12)
         squares(11)
-        q_pz(15)
         finish(10)
         xbias(12)
         store(10)
@@ -527,6 +518,7 @@ def tile_softmaxattention_pb_t_kernel(tc, attn, pz, Wo_bytes, Wo_scale, bo, x, g
         stage1(15, 3)
         add(12)
         center(11)
+        negmean(12)
         ymm(13)
         squares(12)
         finish(11)
@@ -536,6 +528,7 @@ def tile_softmaxattention_pb_t_kernel(tc, attn, pz, Wo_bytes, Wo_scale, bo, x, g
         rstd(12)
         add(13)
         center(12)
+        negmean(13)
         ymm(14)
         squares(13)
         finish(12)
@@ -544,6 +537,7 @@ def tile_softmaxattention_pb_t_kernel(tc, attn, pz, Wo_bytes, Wo_scale, bo, x, g
         rstd(13)
         add(14)
         center(13)
+        negmean(14)
         ymm(15)
         squares(14)
         finish(13)
@@ -552,6 +546,7 @@ def tile_softmaxattention_pb_t_kernel(tc, attn, pz, Wo_bytes, Wo_scale, bo, x, g
         rstd(14)
         add(15)
         center(14)
+        negmean(15)
         squares(15)
         finish(14)
         store(14)

from contextlib import ExitStack

import concourse.mybir as mybir
from concourse.masks import make_identity

B, HEADS, T, D = 8, 2, 512, 512
FLOPS = 2 * B * HEADS * T * T * D + 2 * B * T * HEADS * D * D

F32 = mybir.dt.float32
BF16 = mybir.dt.bfloat16
U32 = mybir.dt.uint32
U8 = mybir.dt.uint8
FP8 = mybir.dt.float8_e4m3fn
FP8X4 = mybir.dt.float8_e4m3fn_x4
ALU = mybir.AluOpType
ACT = mybir.ActivationFunctionType

P = 128
N_HEADS = B * HEADS
PE_PAIRS = (4, 5, 6, 7, 8, 9, 10, 11, 12, 13, 14, 15)
LEAD = 4


def tile_softmaxattention_pb_t_kernel(tc, attn, pz, Wo_bytes, Wo_scale, bo, x, gamma, beta, out):
    nc = tc.nc
    with ExitStack() as ctx:
        const = ctx.enter_context(tc.tile_pool(name="const", bufs=1))
        raw = ctx.enter_context(tc.tile_pool(name="raw", bufs=6))
        grp = ctx.enter_context(tc.tile_pool(name="grp", bufs=3))
        codes = ctx.enter_context(tc.tile_pool(name="codes", bufs=3))
        ccodes = ctx.enter_context(tc.tile_pool(name="ccodes", bufs=5))
        post = ctx.enter_context(tc.tile_pool(name="post", bufs=3))
        small = ctx.enter_context(tc.tile_pool(name="small", bufs=4))
        ps_tr = ctx.enter_context(tc.psum_pool(name="ps_tr", bufs=2))
        ps_cat = ctx.enter_context(tc.psum_pool(name="ps_cat", bufs=4))
        ps_y = ctx.enter_context(tc.psum_pool(name="ps_y", bufs=2))

        ident_f = const.tile([P, P], F32, align_bytes=64)
        ident_b = const.tile([P, P], BF16, align_bytes=64)
        make_identity(nc, ident_f[:])
        make_identity(nc, ident_b[:])
        row0 = const.tile([P, P], BF16, align_bytes=64)
        nc.gpsimd.memset(row0[:], 0.0)
        nc.gpsimd.memset(row0[0:1, :], 1.0)

        wo_raw = const.tile([P, 4, HEADS * D], U8, align_bytes=64)
        wo_sc = const.tile([P, HEADS * D], F32, align_bytes=64)
        wo_w = const.tile([P, 4, HEADS * D], BF16, align_bytes=64)
        wo_p = const.tile([P, 4, HEADS, 4, P], BF16, align_bytes=64)
        wo_grp = const.tile([P, HEADS, D, 4], BF16, align_bytes=64)
        wo_codes = const.tile([P, HEADS, D], U32, align_bytes=64)
        wo_scales = const.tile([P, HEADS, D], U8, align_bytes=64)
        bo_t = const.tile([P, D], BF16, align_bytes=64)
        gamma_t = const.tile([P, D], BF16, align_bytes=64)
        beta_t = const.tile([P, D], BF16, align_bytes=64)

        attn_h = attn.rearrange("b m (p j) s -> (b m) p (j s)", j=4)
        pz_h = pz.rearrange("b m (p j) i -> (b m) p (j i)", j=4)
        x_b = x.rearrange("b (p j) o -> b p j o", j=4)
        out_b = out.rearrange("b (p j) o -> b p j o", j=4)

        st = {}

        def load_pz(n):
            t = raw.tile([P, 4 * D], BF16, align_bytes=64, name="pz_raw")
            nc.sync.dma_start(out=t[:], in_=pz_h[n])
            st["pz_raw", n] = t

        def load_attn(n):
            t = raw.tile([P, 4 * T], BF16, align_bytes=64, name="attn_raw")
            nc.sync.dma_start(out=t[:], in_=attn_h[n])
            st["attn_raw", n] = t

        def load_x(b):
            t = post.tile([P, 4, D], BF16, align_bytes=64, name="x_raw")
            nc.sync.dma_start(out=t[:], in_=x_b[b])
            st["x", b] = t

        def attn_turn(n):
            words = st["attn_raw", n][:].bitcast(F32)
            both = grp.tile([P, 2, 4 * D], BF16, align_bytes=64, name="in_g")
            st["in_g", n] = both
            gw = both[:, 0, :].bitcast(F32).rearrange("p (a r u) -> p a r u", a=4, u=2)
            for h in range(2):
                bank = ps_tr.tile([P, 2, 2, P], F32, name="tr")
                for a in range(2):
                    j = 2 * h + a
                    for u in range(2):
                        nc.tensor.transpose(bank[:, a, u, :], words[:, 256 * j + u : 256 * (j + 1) : 2], ident_f[:])
                nc.scalar.copy(out=gw[:, 2 * h : 2 * h + 2], in_=bank[:].rearrange("p a u r -> p a r u"))

        def pz_lay(n):
            src = st["pz_raw", n][:].rearrange("p (j b t i) -> p b t j i", j=4, b=32, t=4)
            dst = st["in_g", n][:, 1, :].rearrange("p (t b i j) -> p b t j i", t=4, b=32, i=4)
            nc.vector.tensor_copy(out=dst, in_=src)

        def q_in(n):
            c = codes.tile([P, 2, 512], U32, align_bytes=64, name="in_c")
            s = codes.tile([P, 2, 512], U8, align_bytes=64, name="in_s")
            nc.vector.quantize_mx(out=c[:].rearrange("p a w -> p (a w)").bitcast(FP8X4), scales=s[:].rearrange("p a w -> p (a w)"),
                                  in_=st["in_g", n][:].rearrange("p a w -> p (a w)"))
            st["in_q", n] = (c, s)

        def q_cat(n):
            c = ccodes.tile([P, 512], U32, align_bytes=64, name="cat_c")
            s = ccodes.tile([P, 512], U8, align_bytes=64, name="cat_s")
            nc.vector.quantize_mx(out=c[:].bitcast(FP8X4), scales=s[:], in_=st["cat_g", n][:].rearrange("p c t -> p (c t)"))
            st["cat_q", n] = (c, s)

        def stage1(n, j):
            if j == 0:
                st["cat_g", n] = grp.tile([P, T, 4], BF16, align_bytes=64, name="cat_g")
            ic, isc = st["in_q", n]
            cols = slice(P * j, P * (j + 1))
            bank = ps_cat.tile([P, 4, P], F32, name="catb")
            for t in range(4):
                ch = slice(P * t, P * (t + 1))
                nc.tensor.matmul_mx(
                    out=bank[:, t, :], lhsT=ic[:, 1, ch].bitcast(FP8X4), lhsT_scale=isc[:, 1, ch],
                    rhs=ic[:, 0, cols].bitcast(FP8X4), rhs_scale=isc[:, 0, cols], start=True, stop=True)
            nc.scalar.copy(out=st["cat_g", n][:, cols, :], in_=bank[:].rearrange("p t c -> p c t"))

        def wo_scale(q):
            nc.vector.tensor_tensor(out=wo_w[:, q, :], in0=wo_raw[:, q, :].bitcast(FP8), in1=wo_sc[:], op=ALU.mult)

        def wo_order(q):
            for g in range(HEADS):
                nc.scalar.copy(
                    out=wo_p[:, q, g].rearrange("p t (b i) -> p t b i", b=32),
                    in_=wo_w[:, q, D * g : D * (g + 1)].rearrange("p (b t i) -> p t b i", b=32, t=4))

        def wo_turn(q):
            bank = ps_tr.tile([P, HEADS, 4, P], BF16, name="tr")
            for g in range(HEADS):
                for t in range(4):
                    nc.tensor.transpose(bank[:, g, t, :], wo_p[:, q, g, t, :], ident_b[:])
            nc.scalar.copy(out=wo_grp[:, :, P * q : P * (q + 1), :], in_=bank[:].rearrange("p g t o -> p g o t"))

        def wo_quant(g):
            nc.vector.quantize_mx(out=wo_codes[:, g, :].bitcast(FP8X4), scales=wo_scales[:, g, :],
                                  in_=wo_grp[:, g].rearrange("p c t -> p (c t)"))

        def ymm(q):
            b, h = divmod(q, 2)
            banks = []
            for a in range(2):
                cols = slice(P * (2 * h + a), P * (2 * h + a + 1))
                bank = ps_y.tile([P, D], F32, name="yb")
                for m in range(2):
                    cc, cs = st["cat_q", 2 * b + m]
                    nc.tensor.matmul_mx(
                        out=bank[:], lhsT=cc[:, cols].bitcast(FP8X4), lhsT_scale=cs[:, cols],
                        rhs=wo_codes[:, m, :].bitcast(FP8X4), rhs_scale=wo_scales[:, m, :],
                        start=(m == 0), stop=(m == 1))
                banks.append(bank)
            st["y", q] = banks

        def xbias(q):
            b, h = divmod(q, 2)
            t = post.tile([P, 2, D], F32, align_bytes=64, name="xb")
            st["xb", q] = t
            if q in PE_PAIRS:
                for a in range(2):
                    bank = ps_tr.tile([P, D], F32, name="tr")
                    nc.tensor.matmul(out=bank[:], lhsT=ident_b[:], rhs=st["x", b][:, 2 * h + a, :], start=True, stop=False)
                    nc.tensor.matmul(out=bank[:], lhsT=row0[:], rhs=bo_t[:], start=False, stop=True)
                    nc.scalar.copy(out=t[:, a, :], in_=bank[:])
                return
            nc.vector.tensor_tensor(out=t[:], in0=st["x", b][:, 2 * h : 2 * h + 2, :],
                                    in1=bo_t[:].unsqueeze(1).to_broadcast([P, 2, D]), op=ALU.add)

        def add(q):
            xb = st["xb", q]
            h = post.tile([P, 2, D], F32, align_bytes=64, name="h")
            sm = small.tile([P, 2], F32, name="sm")
            for a in range(2):
                nc.vector.scalar_tensor_tensor(out=h[:, a, :], in0=st["y", q][a][:], scalar=1.0, in1=xb[:, a, :],
                                               op0=ALU.mult, op1=ALU.add, accum_out=sm[:, a : a + 1])
            st["sm", q] = sm
            st["hh", q] = h

        def negmean(q):
            nm = small.tile([P, 2], F32, name="nm")
            nc.scalar.activation(out=nm[:], in_=st["sm", q][:], func=ACT.Copy, scale=-1.0 / D)
            st["h", q] = (st["hh", q], nm)

        def squares(q):
            h, nm = st["h", q]
            ss = small.tile([P, 2], F32, name="ss")
            for a in range(2):
                junk = post.tile([P, D], BF16, align_bytes=64, name="junk")
                nc.scalar.activation(out=junk[:], in_=h[:, a, :], func=ACT.Square, bias=nm[:, a : a + 1],
                                     accum_out=ss[:, a : a + 1])
            st["ss", q] = ss

        def rstd(q):
            rs = small.tile([P, 2], F32, name="rs")
            nc.scalar.activation(out=rs[:], in_=st["ss", q][:], func=ACT.Abs_reciprocal_sqrt, scale=1.0 / D, bias=1e-5)
            st["rs", q] = rs

        def center(q):
            h, nm = st["h", q]
            for a in range(2):
                nc.vector.scalar_tensor_tensor(out=h[:, a, :], in0=h[:, a, :], scalar=nm[:, a : a + 1], in1=gamma_t[:],
                                               op0=ALU.add, op1=ALU.mult)

        def finish(q):
            b, half = divmod(q, 2)
            h, nm = st["h", q]
            rs = st["rs", q]
            o = post.tile([P, 2, D], F32, align_bytes=64, name="o")
            for a in range(2):
                nc.vector.scalar_tensor_tensor(out=o[:, a, :], in0=h[:, a, :], scalar=rs[:, a : a + 1], in1=beta_t[:],
                                               op0=ALU.mult, op1=ALU.add)
            st["o", q] = o

        def store(q):
            b, half = divmod(q, 2)
            if q < N_HEADS - 1:
                nc.sync.dma_start(out=out_b[b, :, 2 * half : 2 * half + 2, :], in_=st["o", q][:])
            else:
                for a in range(2):
                    nc.sync.dma_start(out=out_b[b, :, 2 * half + a, :], in_=st["o", q][:, a, :])

        ctx.enter_context(tc.manual_schedule())
        load_attn(0)
        load_pz(0)
        load_attn(1)
        load_pz(1)
        load_attn(2)
        load_pz(2)
        nc.sync.dma_start(out=wo_sc[:], in_=Wo_scale.rearrange("o k -> (o k)").partition_broadcast(P))
        nc.sync.dma_start(out=wo_raw[:], in_=Wo_bytes.rearrange("(q p) k -> p q k", p=P))
        load_x(0)
        nc.sync.dma_start(out=bo_t[:], in_=bo.partition_broadcast(P))
        load_attn(3)
        load_pz(3)
        nc.sync.dma_start(out=gamma_t[:], in_=gamma.partition_broadcast(P))
        nc.sync.dma_start(out=beta_t[:], in_=beta.partition_broadcast(P))
        load_x(1)
        load_attn(4)
        load_pz(4)
        load_attn(5)
        load_pz(5)
        load_attn(6)
        load_pz(6)
        attn_turn(0)
        pz_lay(0)
        attn_turn(1)
        q_in(0)
        pz_lay(1)
        q_in(1)
        stage1(0, 0)
        stage1(0, 1)
        stage1(0, 2)
        stage1(0, 3)
        wo_scale(0)
        wo_scale(1)
        wo_scale(2)
        wo_scale(3)
        attn_turn(2)
        pz_lay(2)
        stage1(1, 0)
        stage1(1, 1)
        wo_order(0)
        wo_order(1)
        wo_order(2)
        wo_order(3)
        stage1(1, 2)
        stage1(1, 3)
        q_in(2)
        wo_turn(0)
        wo_turn(1)
        wo_turn(2)
        wo_turn(3)
        attn_turn(3)
        xbias(0)
        pz_lay(3)
        q_cat(0)
        wo_quant(0)
        wo_quant(1)
        load_x(2)
        q_cat(1)
        stage1(2, 0)
        stage1(2, 1)
        stage1(2, 2)
        stage1(2, 3)
        q_in(3)
        attn_turn(4)
        ymm(0)
        pz_lay(4)
        load_attn(7)
        load_pz(7)
        q_cat(2)
        stage1(3, 0)
        stage1(3, 1)
        stage1(3, 2)
        stage1(3, 3)
        add(0)
        q_in(4)
        negmean(0)
        attn_turn(5)
        ymm(1)
        squares(0)
        pz_lay(5)
        xbias(1)
        load_attn(8)
        load_pz(8)
        load_x(3)
        q_cat(3)
        stage1(4, 0)
        rstd(0)
        stage1(4, 1)
        stage1(4, 2)
        stage1(4, 3)
        add(1)
        q_in(5)
        center(0)
        negmean(1)
        attn_turn(6)
        ymm(2)
        squares(1)
        finish(0)
        pz_lay(6)
        xbias(2)
        load_attn(9)
        load_pz(9)
        store(0)
        q_cat(4)
        stage1(5, 0)
        rstd(1)
        stage1(5, 1)
        stage1(5, 2)
        stage1(5, 3)
        add(2)
        q_in(6)
        center(1)
        negmean(2)
        attn_turn(7)
        ymm(3)
        squares(2)
        finish(1)
        pz_lay(7)
        xbias(3)
        load_attn(10)
        load_pz(10)
        load_x(4)
        store(1)
        q_cat(5)
        stage1(6, 0)
        rstd(2)
        stage1(6, 1)
        stage1(6, 2)
        stage1(6, 3)
        add(3)
        q_in(7)
        center(2)
        negmean(3)
        attn_turn(8)
        ymm(4)
        squares(3)
        finish(2)
        pz_lay(8)
        xbias(4)
        load_attn(11)
        load_pz(11)
        store(2)
        q_cat(6)
        stage1(7, 0)
        rstd(3)
        stage1(7, 1)
        stage1(7, 2)
        stage1(7, 3)
        add(4)
        q_in(8)
        center(3)
        negmean(4)
        attn_turn(9)
        ymm(5)
        squares(4)
        finish(3)
        pz_lay(9)
        xbias(5)
        load_attn(12)
        load_pz(12)
        load_x(5)
        store(3)
        q_cat(7)
        stage1(8, 0)
        rstd(4)
        stage1(8, 1)
        stage1(8, 2)
        stage1(8, 3)
        add(5)
        q_in(9)
        center(4)
        negmean(5)
        attn_turn(10)
        ymm(6)
        squares(5)
        finish(4)
        pz_lay(10)
        xbias(6)
        load_attn(13)
        load_pz(13)
        store(4)
        q_cat(8)
        stage1(9, 0)
        rstd(5)
        stage1(9, 1)
        stage1(9, 2)
        stage1(9, 3)
        add(6)
        q_in(10)
        center(5)
        negmean(6)
        attn_turn(11)
        ymm(7)
        squares(6)
        finish(5)
        pz_lay(11)
        xbias(7)
        load_attn(14)
        load_pz(14)
        load_x(6)
        store(5)
        q_cat(9)
        stage1(10, 0)
        rstd(6)
        stage1(10, 1)
        stage1(10, 2)
        stage1(10, 3)
        add(7)
        q_in(11)
        center(6)
        negmean(7)
        attn_turn(12)
        ymm(8)
        squares(7)
        finish(6)
        pz_lay(12)
        xbias(8)
        load_attn(15)
        load_pz(15)
        store(6)
        q_cat(10)
        stage1(11, 0)
        rstd(7)
        stage1(11, 1)
        stage1(11, 2)
        stage1(11, 3)
        add(8)
        q_in(12)
        center(7)
        negmean(8)
        attn_turn(13)
        ymm(9)
        squares(8)
        finish(7)
        pz_lay(13)
        xbias(9)
        load_x(7)
        store(7)
        q_cat(11)
        stage1(12, 0)
        rstd(8)
        stage1(12, 1)
        stage1(12, 2)
        stage1(12, 3)
        add(9)
        q_in(13)
        center(8)
        negmean(9)
        attn_turn(14)
        ymm(10)
        squares(9)
        finish(8)
        pz_lay(14)
        xbias(10)
        store(8)
        q_cat(12)
        stage1(13, 0)
        rstd(9)
        stage1(13, 1)
        stage1(13, 2)
        stage1(13, 3)
        add(10)
        q_in(14)
        center(9)
        negmean(10)
        attn_turn(15)
        ymm(11)
        squares(10)
        finish(9)
        pz_lay(15)
        xbias(11)
        store(9)
        q_cat(13)
        stage1(14, 0)
        rstd(10)
        stage1(14, 1)
        stage1(14, 2)
        stage1(14, 3)
        add(11)
        q_in(15)
        center(10)
        negmean(11)
        ymm(12)
        squares(11)
        finish(10)
        xbias(12)
        store(10)
        q_cat(14)
        stage1(15, 0)
        rstd(11)
        stage1(15, 1)
        stage1(15, 2)
        stage1(15, 3)
        add(12)
        center(11)
        negmean(12)
        ymm(13)
        squares(12)
        finish(11)
        xbias(13)
        store(11)
        q_cat(15)
        rstd(12)
        add(13)
        center(12)
        negmean(13)
        ymm(14)
        squares(13)
        finish(12)
        xbias(14)
        store(12)
        rstd(13)
        add(14)
        center(13)
        negmean(14)
        ymm(15)
        squares(14)
        finish(13)
        xbias(15)
        store(13)
        rstd(14)
        add(15)
        center(14)
        negmean(15)
        squares(15)
        finish(14)
        store(14)
        rstd(15)
        center(15)
        finish(15)
        store(15)
